import numpy as np
import ml_dtypes


def mxq(x, axis, fmt="e4m3"):
    dtype, down = {"e4m3": (ml_dtypes.float8_e4m3fn, 7), "e5m2": (ml_dtypes.float8_e5m2, 14)}[fmt]
    v = np.moveaxis(np.asarray(x, np.float32).astype(ml_dtypes.bfloat16).astype(np.float64), axis, -1)
    blocks = v.reshape(v.shape[:-1] + (-1, 32))
    amax = np.abs(blocks).max(-1, keepdims=True)
    byte = np.maximum(np.where(amax > 0, np.frexp(amax)[1] - 1 + 127, 0) - down, 1)
    scale = np.exp2(byte - 127.0)
    codes = (blocks / scale).astype(np.float32).astype(dtype).astype(np.float64)
    return np.moveaxis((codes * scale).reshape(v.shape), -1, axis)


WIDE = False


def mx_kscale(k):
    if not WIDE:
        return np.ones(k)
    levels = np.array([20, -20, 10, -10, 0])
    a = np.random.permutation(np.resize(levels, k // 512 * 4)).reshape(k // 512, 4)
    idx = np.arange(k)
    return np.exp2(a[idx // 512, idx % 128 // 32])


BF16 = ml_dtypes.bfloat16


def bf(x):
    return np.asarray(x, np.float32).astype(BF16)


def f64(x):
    return np.asarray(x).astype(np.float64)


H, W, C = 64, 48, 512
HW = H * W


def setup_inputs():
    s = mx_kscale(HW)
    weights = np.random.uniform(0.0, 1.0, (HW, H, W)) * 0.03 * s[:, None, None]
    cnn_feature = np.random.standard_normal((1, C, H, W))
    g = np.random.standard_normal((HW, 1, 1, C)) * np.exp2(np.random.randint(-12, 1, (HW, 1, 1, 1))) * 4.0 / s[:, None, None, None]
    return {"weights": bf(weights), "cnn_feature": bf(cnn_feature), "grad_out": bf(g)}


def reference(weights, cnn_feature, grad_out):
    b, c, h, w = cnn_feature.shape
    hw = h * w
    attn = f64(weights).reshape(hw, hw)
    g = f64(grad_out).reshape(hw, c)
    d = mxq(g, 0, "e5m2").T @ mxq(attn, 0, "e4m3")
    return d.reshape(1, c, h, w)

@@ -1,0 +1,177 @@
+from contextlib import ExitStack
+
+import concourse.mybir as mybir
+
+BF16 = mybir.dt.bfloat16
+F32 = mybir.dt.float32
+U32 = mybir.dt.uint32
+U8 = mybir.dt.uint8
+E4 = mybir.dt.float8_e4m3fn_x4
+E5 = mybir.dt.float8_e5m2_x4
+
+P = 128
+PACK = 4
+K_PASS = P * PACK
+K = 3072
+C = 512
+N = 3072
+PASSES = K // K_PASS
+N_TILE = 512
+BLOCK = 1024
+BLOCKS = N // BLOCK
+M_TILES = C // P
+
+FLOPS = 2 * C * K * N
+BYTES = 2 * K * N + 2 * K * C + 4 * C * N
+
+PINNED = True
+V_SHARE = 0.5625
+TAIL_SHARE = 0.65625
+RAW_BUFS = 10
+GRP_BUFS = 4
+CODE_BUFS = 3
+Q_LAG = 2
+
+
+def tile_attention_weighted_context_generation_kernel(tc, weights, cnn_feature, grad_out, out):
+    nc = tc.nc
+    w2 = weights.rearrange("p h w -> p (h w)")
+    g2 = grad_out.rearrange("p a b c -> p (a b c)")
+    o2 = out.rearrange("o c h w -> (o c) (h w)")
+
+    pieces = []
+    for c in range(PASSES):
+        pieces.append(("g", 0, c))
+        pieces.append(("w", 0, c))
+    for b in range(1, BLOCKS):
+        for c in range(PASSES):
+            pieces.append(("w", b, c))
+    n_pieces = len(pieces)
+
+    with ExitStack() as ctx:
+        if PINNED:
+            ctx.enter_context(tc.manual_schedule())
+        raw_pool = ctx.enter_context(tc.tile_pool(name="raw", bufs=RAW_BUFS))
+        grp_pool = ctx.enter_context(tc.tile_pool(name="grp", bufs=GRP_BUFS))
+        code_pool = ctx.enter_context(tc.tile_pool(name="code", bufs=CODE_BUFS))
+        keep = ctx.enter_context(tc.tile_pool(name="keep", bufs=1))
+        stage_pool = ctx.enter_context(tc.tile_pool(name="stage", bufs=BLOCKS * M_TILES))
+        psum = ctx.enter_context(tc.psum_pool(name="acc", bufs=1))
+
+        g_codes = []
+        g_scales = []
+        for c in range(PASSES):
+            g_codes.append(keep.tile([P, C], U32, name="gq%d" % c, align_bytes=64))
+            g_scales.append(keep.tile([P, C], U8, name="gs%d" % c, align_bytes=64))
+
+        raws = {}
+        grps = {}
+        accs = {}
+        stages = {}
+
+        def width(s):
+            return C if pieces[s][0] == "g" else BLOCK
+
+        def load(s):
+            kind, b, c = pieces[s]
+            raw = raw_pool.tile([P, PACK, width(s)], BF16, name="raw%d" % s, tag="raw")
+            rows = slice(c * K_PASS, (c + 1) * K_PASS)
+            if kind == "g":
+                src = g2[rows, :]
+            else:
+                src = w2[rows, b * BLOCK:(b + 1) * BLOCK]
+            nc.sync.dma_start(out=raw[:], in_=src.rearrange("(p j) w -> p j w", j=PACK))
+            raws[s] = raw
+
+        def regroup(engine, s, x0, x1):
+            dst = grps[s][:, x0:x1, :].rearrange("p (c i) t -> p c t i", i=4)
+            src = raws[s][:, :, x0:x1].rearrange("p t (c i) -> p c t i", i=4)
+            if engine == "v":
+                nc.vector.tensor_copy(out=dst, in_=src)
+            else:
+                nc.scalar.copy(out=dst, in_=src)
+
+        def copies(s):
+            w = width(s)
+            grps[s] = grp_pool.tile([P, w, PACK], BF16, name="grp%d" % s, tag="grp", align_bytes=64)
+            if s == n_pieces - 1:
+                a = int(N_TILE * TAIL_SHARE) // 8 * 8
+                for h in range(2):
+                    regroup("v", s, h * N_TILE, h * N_TILE + a)
+                    regroup("s", s, h * N_TILE + a, (h + 1) * N_TILE)
+            else:
+                a = int(w * V_SHARE) // 8 * 8
+                regroup("v", s, 0, a)
+                regroup("s", s, a, w)
+
+        def quantise(s):
+            kind, b, c = pieces[s]
+            flat = grps[s][:].rearrange("p w j -> p (w j)")
+            if kind == "g":
+                nc.vector.quantize_mx(out=g_codes[c][:].bitcast(E5), scales=g_scales[c][:], in_=flat)
+                return None
+            codes = code_pool.tile([P, BLOCK], U32, name="wq%d" % s, tag="wq", align_bytes=64)
+            scales = code_pool.tile([P, BLOCK], U8, name="ws%d" % s, tag="ws", align_bytes=64)
+            if s == n_pieces - 1:
+                for h in range(2):
+                    cols = slice(h * N_TILE, (h + 1) * N_TILE)
+                    nc.vector.quantize_mx(
+                        out=codes[:, cols].bitcast(E4),
+                        scales=scales[:, cols],
+                        in_=flat[:, h * N_TILE * PACK:(h + 1) * N_TILE * PACK],
+                    )
+            else:
+                nc.vector.quantize_mx(out=codes[:].bitcast(E4), scales=scales[:], in_=flat)
+            return codes, scales
+
+        def passes(s, codes, scales):
+            kind, b, c = pieces[s]
+            for h in range(2):
+                cols = slice(h * N_TILE, (h + 1) * N_TILE)
+                for m in range(M_TILES):
+                    if c == 0:
+                        accs[(h, m)] = psum.tile([P, N_TILE], F32, name="acc%d_%d%d" % (b, h, m), tag="acc%d%d" % (h, m))
+                    acc = accs[(h, m)]
+                    mc = slice(m * P, (m + 1) * P)
+                    nc.tensor.matmul_mx(
+                        out=acc[:],
+                        lhsT=g_codes[c][:, mc].bitcast(E5),
+                        lhsT_scale=g_scales[c][:, mc],
+                        rhs=codes[:, cols].bitcast(E4),
+                        rhs_scale=scales[:, cols],
+                        start=(c == 0),
+                        stop=(c == PASSES - 1),
+                    )
+                    if c == PASSES - 1:
+                        if h == 0:
+                            stages[(b, m)] = stage_pool.tile([P, BLOCK], F32, name="st%d_%d" % (b, m), tag="st")
+                        dst = stages[(b, m)][:, cols]
+                        if b == BLOCKS - 1 and m % 2 == 1:
+                            nc.vector.tensor_copy(out=dst, in_=acc[:])
+                        else:
+                            nc.scalar.copy(out=dst, in_=acc[:])
+
+        ahead = RAW_BUFS - 1
+        for s in range(ahead):
+            load(s)
+        for s in range(n_pieces + Q_LAG):
+            if s + ahead < n_pieces:
+                load(s + ahead)
+            if s < n_pieces:
+                copies(s)
+            i = s - Q_LAG
+            if 0 <= i < n_pieces:
+                got = quantise(i)
+                if got is not None:
+                    passes(i, got[0], got[1])
+
+        for b in range(BLOCKS - 1):
+            for m in range(M_TILES):
+                nc.sync.dma_start(out=o2[m * P:(m + 1) * P, b * BLOCK:(b + 1) * BLOCK], in_=stages[(b, m)][:])
+        b = BLOCKS - 1
+        for h in range(2):
+            for m in range(M_TILES):
+                nc.sync.dma_start(
+                    out=o2[m * P:(m + 1) * P, b * BLOCK + h * N_TILE:b * BLOCK + (h + 1) * N_TILE],
+                    in_=stages[(b, m)][:, h * N_TILE:(h + 1) * N_TILE],
+                )

@@ -20,17 +20,21 @@ N_TILE = 512
 BLOCK = 1024
 BLOCKS = N // BLOCK
 M_TILES = C // P
+LAST_TILE = N // N_TILE - 1
 
 FLOPS = 2 * C * K * N
 BYTES = 2 * K * N + 2 * K * C + 4 * C * N
 
 PINNED = True
-V_SHARE = 0.5625
-TAIL_SHARE = 0.65625
+F_NORMAL = 0.5
+F_AFTER = 0.75
+F_TAIL = 0.5
 RAW_BUFS = 10
-GRP_BUFS = 4
+GRP_BUFS = 6
 CODE_BUFS = 3
 Q_LAG = 2
+HEAD_SPLIT = True
+TAIL_CHUNKS = 2
 
 
 def tile_attention_weighted_context_generation_kernel(tc, weights, cnn_feature, grad_out, out):
@@ -39,14 +43,37 @@ def tile_attention_weighted_context_generation_kernel(tc, weights, cnn_feature, 
     g2 = grad_out.rearrange("p a b c -> p (a b c)")
     o2 = out.rearrange("o c h w -> (o c) (h w)")
 
-    pieces = []
+    loads = []
+    works = []
+
+    def add_load(kind, c, col0, cols):
+        loads.append((kind, c, col0, cols))
+        return len(loads) - 1
+
     for c in range(PASSES):
-        pieces.append(("g", 0, c))
-        pieces.append(("w", 0, c))
+        works.append((add_load("g", c, 0, C), "g", c, 0, C, F_NORMAL))
+        if c == 0 and HEAD_SPLIT:
+            for h in range(2):
+                works.append((add_load("w", c, h * N_TILE, N_TILE), "w", c, 0, N_TILE, F_NORMAL))
+        else:
+            works.append((add_load("w", c, 0, BLOCK), "w", c, 0, BLOCK, F_NORMAL))
+    tail_loads = []
     for b in range(1, BLOCKS):
         for c in range(PASSES):
-            pieces.append(("w", b, c))
-    n_pieces = len(pieces)
+            ld = add_load("w", c, b * BLOCK, BLOCK)
+            if b == BLOCKS - 1 and c >= PASSES - TAIL_CHUNKS:
+                tail_loads.append((ld, c))
+            else:
+                share = F_AFTER if c in (Q_LAG, Q_LAG + 1) else F_NORMAL
+                works.append((ld, "w", c, 0, BLOCK, share))
+    for h in range(2):
+        for ld, c in tail_loads:
+            works.append((ld, "w", c, h * N_TILE, N_TILE, F_TAIL))
+    n_works = len(works)
+    n_loads = len(loads)
+    last_work_of = {}
+    for i in range(n_works):
+        last_work_of[works[i][0]] = i
 
     with ExitStack() as ctx:
         if PINNED:
@@ -69,101 +96,76 @@ def tile_attention_weighted_context_generation_kernel(tc, weights, cnn_feature, 
         accs = {}
         stages = {}
 
-        def width(s):
-            return C if pieces[s][0] == "g" else BLOCK
-
-        def load(s):
-            kind, b, c = pieces[s]
-            raw = raw_pool.tile([P, PACK, width(s)], BF16, name="raw%d" % s, tag="raw")
+        def load(ld):
+            kind, c, col0, cols = loads[ld]
+            raw = raw_pool.tile([P, PACK, cols], BF16, name="raw%d" % ld, tag="raw")
             rows = slice(c * K_PASS, (c + 1) * K_PASS)
-            if kind == "g":
-                src = g2[rows, :]
-            else:
-                src = w2[rows, b * BLOCK:(b + 1) * BLOCK]
+            src = g2[rows, :] if kind == "g" else w2[rows, col0:col0 + cols]
             nc.sync.dma_start(out=raw[:], in_=src.rearrange("(p j) w -> p j w", j=PACK))
-            raws[s] = raw
+            raws[ld] = raw
 
-        def regroup(engine, s, x0, x1):
-            dst = grps[s][:, x0:x1, :].rearrange("p (c i) t -> p c t i", i=4)
-            src = raws[s][:, :, x0:x1].rearrange("p t (c i) -> p c t i", i=4)
-            if engine == "v":
+        def regroup(on_vector, i, x0, x1):
+            ld, kind, c, off, cols, share = works[i]
+            dst = grps[i][:, x0:x1, :].rearrange("p (c i) t -> p c t i", i=4)
+            src = raws[ld][:, :, off + x0:off + x1].rearrange("p t (c i) -> p c t i", i=4)
+            if on_vector:
                 nc.vector.tensor_copy(out=dst, in_=src)
             else:
                 nc.scalar.copy(out=dst, in_=src)
 
-        def copies(s):
-            w = width(s)
-            grps[s] = grp_pool.tile([P, w, PACK], BF16, name="grp%d" % s, tag="grp", align_bytes=64)
-            if s == n_pieces - 1:
-                a = int(N_TILE * TAIL_SHARE) // 8 * 8
-                for h in range(2):
-                    regroup("v", s, h * N_TILE, h * N_TILE + a)
-                    regroup("s", s, h * N_TILE + a, (h + 1) * N_TILE)
-            else:
-                a = int(w * V_SHARE) // 8 * 8
-                regroup("v", s, 0, a)
-                regroup("s", s, a, w)
+        def copies(i):
+            ld, kind, c, off, cols, share = works[i]
+            grps[i] = grp_pool.tile([P, cols, PACK], BF16, name="grp%d" % i, tag="grp", align_bytes=64)
+            a = int(cols * share) // 8 * 8
+            regroup(True, i, 0, a)
+            regroup(False, i, a, cols)
 
-        def quantise(s):
-            kind, b, c = pieces[s]
-            flat = grps[s][:].rearrange("p w j -> p (w j)")
+        def quantise_and_multiply(i):
+            ld, kind, c, off, cols, share = works[i]
+            flat = grps[i][:].rearrange("p w j -> p (w j)")
             if kind == "g":
                 nc.vector.quantize_mx(out=g_codes[c][:].bitcast(E5), scales=g_scales[c][:], in_=flat)
-                return None
-            codes = code_pool.tile([P, BLOCK], U32, name="wq%d" % s, tag="wq", align_bytes=64)
-            scales = code_pool.tile([P, BLOCK], U8, name="ws%d" % s, tag="ws", align_bytes=64)
-            if s == n_pieces - 1:
-                for h in range(2):
-                    cols = slice(h * N_TILE, (h + 1) * N_TILE)
-                    nc.vector.quantize_mx(
-                        out=codes[:, cols].bitcast(E4),
-                        scales=scales[:, cols],
-                        in_=flat[:, h * N_TILE * PACK:(h + 1) * N_TILE * PACK],
-                    )
-            else:
-                nc.vector.quantize_mx(out=codes[:].bitcast(E4), scales=scales[:], in_=flat)
-            return codes, scales
-
-        def passes(s, codes, scales):
-            kind, b, c = pieces[s]
-            for h in range(2):
-                cols = slice(h * N_TILE, (h + 1) * N_TILE)
+                return
+            codes = code_pool.tile([P, cols], U32, name="wq%d" % i, tag="wq", align_bytes=64)
+            scales = code_pool.tile([P, cols], U8, name="ws%d" % i, tag="ws", align_bytes=64)
+            nc.vector.quantize_mx(out=codes[:].bitcast(E4), scales=scales[:], in_=flat)
+            col0 = loads[ld][2] + off
+            for u in range(cols // N_TILE):
+                t = col0 // N_TILE + u
+                cs = slice(u * N_TILE, (u + 1) * N_TILE)
                 for m in range(M_TILES):
                     if c == 0:
-                        accs[(h, m)] = psum.tile([P, N_TILE], F32, name="acc%d_%d%d" % (b, h, m), tag="acc%d%d" % (h, m))
-                    acc = accs[(h, m)]
+                        accs[(t, m)] = psum.tile([P, N_TILE], F32, name="acc%d_%d" % (t, m), tag="acc%d%d" % (t % 2, m))
+                    acc = accs[(t, m)]
                     mc = slice(m * P, (m + 1) * P)
                     nc.tensor.matmul_mx(
                         out=acc[:],
                         lhsT=g_codes[c][:, mc].bitcast(E5),
                         lhsT_scale=g_scales[c][:, mc],
-                        rhs=codes[:, cols].bitcast(E4),
-                        rhs_scale=scales[:, cols],
+                        rhs=codes[:, cs].bitcast(E4),
+                        rhs_scale=scales[:, cs],
                         start=(c == 0),
                         stop=(c == PASSES - 1),
                     )
                     if c == PASSES - 1:
-                        if h == 0:
+                        b = t // 2
+                        if (b, m) not in stages:
                             stages[(b, m)] = stage_pool.tile([P, BLOCK], F32, name="st%d_%d" % (b, m), tag="st")
-                        dst = stages[(b, m)][:, cols]
-                        if b == BLOCKS - 1 and m % 2 == 1:
+                        dst = stages[(b, m)][:, (t % 2) * N_TILE:(t % 2 + 1) * N_TILE]
+                        if t == LAST_TILE and m % 2 == 1:
                             nc.vector.tensor_copy(out=dst, in_=acc[:])
                         else:
                             nc.scalar.copy(out=dst, in_=acc[:])
 
-        ahead = RAW_BUFS - 1
-        for s in range(ahead):
-            load(s)
-        for s in range(n_pieces + Q_LAG):
-            if s + ahead < n_pieces:
-                load(s + ahead)
-            if s < n_pieces:
+        next_load = 0
+        for s in range(n_works + Q_LAG):
+            while next_load < n_loads and (next_load < RAW_BUFS or last_work_of[next_load - RAW_BUFS] < s):
+                load(next_load)
+                next_load += 1
+            if s < n_works:
                 copies(s)
-            i = s - Q_LAG
-            if 0 <= i < n_pieces:
-                got = quantise(i)
-                if got is not None:
-                    passes(i, got[0], got[1])
+            if s >= Q_LAG:
+                quantise_and_multiply(s - Q_LAG)
 
         for b in range(BLOCKS - 1):
             for m in range(M_TILES):

@@ -26,7 +26,7 @@ FLOPS = 2 * C * K * N
 BYTES = 2 * K * N + 2 * K * C + 4 * C * N
 
 PINNED = True
-F_NORMAL = 0.5
+F_NORMAL = 0.5625
 F_AFTER = 0.75
 F_TAIL = 0.5
 RAW_BUFS = 10

@@ -21,19 +21,20 @@ BLOCK = 1024
 BLOCKS = N // BLOCK
 M_TILES = C // P
 LAST_TILE = N // N_TILE - 1
+EARLY_TILES = 4
 
 FLOPS = 2 * C * K * N
 BYTES = 2 * K * N + 2 * K * C + 4 * C * N
 
 PINNED = True
-F_NORMAL = 0.5625
+F_NORMAL = 0.5
 F_AFTER = 0.75
 F_TAIL = 0.5
 RAW_BUFS = 10
 GRP_BUFS = 6
 CODE_BUFS = 3
 Q_LAG = 2
-HEAD_SPLIT = True
+HEAD_SPLIT = False
 TAIL_CHUNKS = 2
 
 
@@ -82,7 +83,7 @@ def tile_attention_weighted_context_generation_kernel(tc, weights, cnn_feature, 
         grp_pool = ctx.enter_context(tc.tile_pool(name="grp", bufs=GRP_BUFS))
         code_pool = ctx.enter_context(tc.tile_pool(name="code", bufs=CODE_BUFS))
         keep = ctx.enter_context(tc.tile_pool(name="keep", bufs=1))
-        stage_pool = ctx.enter_context(tc.tile_pool(name="stage", bufs=BLOCKS * M_TILES))
+        stage_pool = ctx.enter_context(tc.tile_pool(name="stage", bufs=M_TILES))
         psum = ctx.enter_context(tc.psum_pool(name="acc", bufs=1))
 
         g_codes = []
@@ -148,10 +149,12 @@ def tile_attention_weighted_context_generation_kernel(tc, weights, cnn_feature, 
                         stop=(c == PASSES - 1),
                     )
                     if c == PASSES - 1:
-                        b = t // 2
-                        if (b, m) not in stages:
-                            stages[(b, m)] = stage_pool.tile([P, BLOCK], F32, name="st%d_%d" % (b, m), tag="st")
-                        dst = stages[(b, m)][:, (t % 2) * N_TILE:(t % 2 + 1) * N_TILE]
+                        late = 1 if t >= EARLY_TILES else 0
+                        if (late, m) not in stages:
+                            wide = (LAST_TILE + 1 - EARLY_TILES if late else EARLY_TILES) * N_TILE
+                            stages[(late, m)] = stage_pool.tile([P, wide], F32, name="st%d_%d" % (late, m), tag="st%d" % late)
+                        u0 = (t - EARLY_TILES if late else t) * N_TILE
+                        dst = stages[(late, m)][:, u0:u0 + N_TILE]
                         if t == LAST_TILE and m % 2 == 1:
                             nc.vector.tensor_copy(out=dst, in_=acc[:])
                         else:
@@ -167,13 +170,12 @@ def tile_attention_weighted_context_generation_kernel(tc, weights, cnn_feature, 
             if s >= Q_LAG:
                 quantise_and_multiply(s - Q_LAG)
 
-        for b in range(BLOCKS - 1):
+        for m in range(M_TILES):
+            nc.sync.dma_start(out=o2[m * P:(m + 1) * P, 0:EARLY_TILES * N_TILE], in_=stages[(0, m)][:])
+        for t in range(EARLY_TILES, LAST_TILE + 1):
             for m in range(M_TILES):
-                nc.sync.dma_start(out=o2[m * P:(m + 1) * P, b * BLOCK:(b + 1) * BLOCK], in_=stages[(b, m)][:])
-        b = BLOCKS - 1
-        for h in range(2):
-            for m in range(M_TILES):
+                u0 = (t - EARLY_TILES) * N_TILE
                 nc.sync.dma_start(
-                    out=o2[m * P:(m + 1) * P, b * BLOCK + h * N_TILE:b * BLOCK + (h + 1) * N_TILE],
-                    in_=stages[(b, m)][:, h * N_TILE:(h + 1) * N_TILE],
+                    out=o2[m * P:(m + 1) * P, t * N_TILE:(t + 1) * N_TILE],
+                    in_=stages[(1, m)][:, u0:u0 + N_TILE],
                 )

from contextlib import ExitStack

import concourse.mybir as mybir

BF16 = mybir.dt.bfloat16
F32 = mybir.dt.float32
U32 = mybir.dt.uint32
U8 = mybir.dt.uint8
E4 = mybir.dt.float8_e4m3fn_x4
E5 = mybir.dt.float8_e5m2_x4

P = 128
PACK = 4
K_PASS = P * PACK
K = 3072
C = 512
N = 3072
PASSES = K // K_PASS
N_TILE = 512
BLOCK = 1024
BLOCKS = N // BLOCK
M_TILES = C // P
LAST_TILE = N // N_TILE - 1
EARLY_TILES = 4

FLOPS = 2 * C * K * N
BYTES = 2 * K * N + 2 * K * C + 4 * C * N

PINNED = True
F_NORMAL = 0.5
F_AFTER = 0.75
F_TAIL = 0.5
RAW_BUFS = 10
GRP_BUFS = 6
CODE_BUFS = 3
Q_LAG = 2
HEAD_SPLIT = False
TAIL_CHUNKS = 2


def tile_attention_weighted_context_generation_kernel(tc, weights, cnn_feature, grad_out, out):
    nc = tc.nc
    w2 = weights.rearrange("p h w -> p (h w)")
    g2 = grad_out.rearrange("p a b c -> p (a b c)")
    o2 = out.rearrange("o c h w -> (o c) (h w)")

    loads = []
    works = []

    def add_load(kind, c, col0, cols):
        loads.append((kind, c, col0, cols))
        return len(loads) - 1

    for c in range(PASSES):
        works.append((add_load("g", c, 0, C), "g", c, 0, C, F_NORMAL))
        if c == 0 and HEAD_SPLIT:
            for h in range(2):
                works.append((add_load("w", c, h * N_TILE, N_TILE), "w", c, 0, N_TILE, F_NORMAL))
        else:
            works.append((add_load("w", c, 0, BLOCK), "w", c, 0, BLOCK, F_NORMAL))
    tail_loads = []
    for b in range(1, BLOCKS):
        for c in range(PASSES):
            ld = add_load("w", c, b * BLOCK, BLOCK)
            if b == BLOCKS - 1 and c >= PASSES - TAIL_CHUNKS:
                tail_loads.append((ld, c))
            else:
                share = F_AFTER if c in (Q_LAG, Q_LAG + 1) else F_NORMAL
                works.append((ld, "w", c, 0, BLOCK, share))
    for h in range(2):
        for ld, c in tail_loads:
            works.append((ld, "w", c, h * N_TILE, N_TILE, F_TAIL))
    n_works = len(works)
    n_loads = len(loads)
    last_work_of = {}
    for i in range(n_works):
        last_work_of[works[i][0]] = i

    with ExitStack() as ctx:
        if PINNED:
            ctx.enter_context(tc.manual_schedule())
        raw_pool = ctx.enter_context(tc.tile_pool(name="raw", bufs=RAW_BUFS))
        grp_pool = ctx.enter_context(tc.tile_pool(name="grp", bufs=GRP_BUFS))
        code_pool = ctx.enter_context(tc.tile_pool(name="code", bufs=CODE_BUFS))
        keep = ctx.enter_context(tc.tile_pool(name="keep", bufs=1))
        stage_pool = ctx.enter_context(tc.tile_pool(name="stage", bufs=M_TILES))
        psum = ctx.enter_context(tc.psum_pool(name="acc", bufs=1))

        g_codes = []
        g_scales = []
        for c in range(PASSES):
            g_codes.append(keep.tile([P, C], U32, name="gq%d" % c, align_bytes=64))
            g_scales.append(keep.tile([P, C], U8, name="gs%d" % c, align_bytes=64))

        raws = {}
        grps = {}
        accs = {}
        stages = {}

        def load(ld):
            kind, c, col0, cols = loads[ld]
            raw = raw_pool.tile([P, PACK, cols], BF16, name="raw%d" % ld, tag="raw")
            rows = slice(c * K_PASS, (c + 1) * K_PASS)
            src = g2[rows, :] if kind == "g" else w2[rows, col0:col0 + cols]
            nc.sync.dma_start(out=raw[:], in_=src.rearrange("(p j) w -> p j w", j=PACK))
            raws[ld] = raw

        def regroup(on_vector, i, x0, x1):
            ld, kind, c, off, cols, share = works[i]
            dst = grps[i][:, x0:x1, :].rearrange("p (c i) t -> p c t i", i=4)
            src = raws[ld][:, :, off + x0:off + x1].rearrange("p t (c i) -> p c t i", i=4)
            if on_vector:
                nc.vector.tensor_copy(out=dst, in_=src)
            else:
                nc.scalar.copy(out=dst, in_=src)

        def copies(i):
            ld, kind, c, off, cols, share = works[i]
            grps[i] = grp_pool.tile([P, cols, PACK], BF16, name="grp%d" % i, tag="grp", align_bytes=64)
            a = int(cols * share) // 8 * 8
            regroup(True, i, 0, a)
            regroup(False, i, a, cols)

        def quantise_and_multiply(i):
            ld, kind, c, off, cols, share = works[i]
            flat = grps[i][:].rearrange("p w j -> p (w j)")
            if kind == "g":
                nc.vector.quantize_mx(out=g_codes[c][:].bitcast(E5), scales=g_scales[c][:], in_=flat)
                return
            codes = code_pool.tile([P, cols], U32, name="wq%d" % i, tag="wq", align_bytes=64)
            scales = code_pool.tile([P, cols], U8, name="ws%d" % i, tag="ws", align_bytes=64)
            nc.vector.quantize_mx(out=codes[:].bitcast(E4), scales=scales[:], in_=flat)
            col0 = loads[ld][2] + off
            for u in range(cols // N_TILE):
                t = col0 // N_TILE + u
                cs = slice(u * N_TILE, (u + 1) * N_TILE)
                for m in range(M_TILES):
                    if c == 0:
                        accs[(t, m)] = psum.tile([P, N_TILE], F32, name="acc%d_%d" % (t, m), tag="acc%d%d" % (t % 2, m))
                    acc = accs[(t, m)]
                    mc = slice(m * P, (m + 1) * P)
                    nc.tensor.matmul_mx(
                        out=acc[:],
                        lhsT=g_codes[c][:, mc].bitcast(E5),
                        lhsT_scale=g_scales[c][:, mc],
                        rhs=codes[:, cs].bitcast(E4),
                        rhs_scale=scales[:, cs],
                        start=(c == 0),
                        stop=(c == PASSES - 1),
                    )
                    if c == PASSES - 1:
                        late = 1 if t >= EARLY_TILES else 0
                        if (late, m) not in stages:
                            wide = (LAST_TILE + 1 - EARLY_TILES if late else EARLY_TILES) * N_TILE
                            stages[(late, m)] = stage_pool.tile([P, wide], F32, name="st%d_%d" % (late, m), tag="st%d" % late)
                        u0 = (t - EARLY_TILES if late else t) * N_TILE
                        dst = stages[(late, m)][:, u0:u0 + N_TILE]
                        if t == LAST_TILE and m % 2 == 1:
                            nc.vector.tensor_copy(out=dst, in_=acc[:])
                        else:
                            nc.scalar.copy(out=dst, in_=acc[:])

        next_load = 0
        for s in range(n_works + Q_LAG):
            while next_load < n_loads and (next_load < RAW_BUFS or last_work_of[next_load - RAW_BUFS] < s):
                load(next_load)
                next_load += 1
            if s < n_works:
                copies(s)
            if s >= Q_LAG:
                quantise_and_multiply(s - Q_LAG)

        for m in range(M_TILES):
            nc.sync.dma_start(out=o2[m * P:(m + 1) * P, 0:EARLY_TILES * N_TILE], in_=stages[(0, m)][:])
        for t in range(EARLY_TILES, LAST_TILE + 1):
            for m in range(M_TILES):
                u0 = (t - EARLY_TILES) * N_TILE
                nc.sync.dma_start(
                    out=o2[m * P:(m + 1) * P, t * N_TILE:(t + 1) * N_TILE],
                    in_=stages[(1, m)][:, u0:u0 + N_TILE],
                )
